import numpy as np
import ml_dtypes

BF16 = ml_dtypes.bfloat16


def bf(x):
    return np.asarray(x, np.float32).astype(BF16)


def f32(x):
    return np.asarray(x, np.float32)


def f64(x):
    return np.asarray(x).astype(np.float64)


def striped(idx):
    return np.tile(idx.reshape(-1, 16).T, (8, 1))


D, S, B, M, N = 1024, 512, 4, 64, 256


def sigmoid(v):
    return 1.0 / (1.0 + np.exp(-v))


def setup_inputs():
    return {'base': f32(0.5 * np.random.standard_normal((D, S))), 'value_clusters': f32(np.random.standard_normal((D, N))), 'vbias': f32(0.1 * np.random.standard_normal((D, M))), 'w': bf(np.random.standard_normal((D, D)) / np.sqrt(D)), 'bv': f32(0.1 * np.random.standard_normal((D, 1))), 'offs': striped(np.random.permutation(S)[:N])}


def reference(base, value_clusters, vbias, w, bv, offs):
    idx = offs[:16].T.reshape(-1)
    cb = f64(value_clusters) + np.tile(f64(vbias), (1, B))
    z = f64(w).T @ cb + f64(bv)
    res = f64(base).copy()
    res[:, idx] = z * sigmoid(z)
    return res

@@ -1,0 +1,70 @@
+import concourse.mybir as mybir
+
+P = 128
+D, S, B, M, N = 1024, 512, 4, 64, 256
+BLOCKS = D // P
+W_PIECES = 4
+FLOPS = 2 * D * D * N
+
+F32, BF16, U16 = mybir.dt.float32, mybir.dt.bfloat16, mybir.dt.uint16
+ADD, MULT = mybir.AluOpType.add, mybir.AluOpType.mult
+SIGMOID, IDENTITY = mybir.ActivationFunctionType.Sigmoid, mybir.ActivationFunctionType.Identity
+
+
+def tile_fuzzyclustering_kernel(tc, base, value_clusters, vbias, w, bv, offs, out):
+    nc = tc.nc
+    with (
+        tc.tile_pool(name="held", bufs=1) as held,
+        tc.tile_pool(name="work", bufs=3) as work,
+        tc.psum_pool(name="psum", bufs=3) as psum,
+    ):
+        offsets = held.tile([P, N // 16], U16, name="offsets")
+        nc.sync.dma_start(offsets[:], offs)
+
+        cluster_bias = held.tile([P, BLOCKS, M], F32, name="cluster_bias")
+        nc.scalar.dma_start(cluster_bias[:], vbias.rearrange("(kb p) m -> p kb m", p=P))
+        clusters = held.tile([P, BLOCKS, N], F32, name="clusters")
+        clusters_dram = value_clusters.rearrange("(kb p) n -> p kb n", p=P)
+        for kb in range(0, BLOCKS, 2):
+            nc.sync.dma_start(clusters[:, kb : kb + 2, :], clusters_dram[:, kb : kb + 2, :])
+
+        layer_bias = held.tile([P, BLOCKS], F32, name="layer_bias")
+        with nc.allow_non_contiguous_dma(reason="1024 single floats, one for each partition and block"):
+            nc.gpsimd.dma_start(layer_bias[:], bv.rearrange("(db p) o -> p (db o)", p=P))
+
+        weights = held.tile([P, BLOCKS, D], BF16, name="weights")
+        weights_dram = w.rearrange("(kb p) d -> p kb d", p=P)
+        piece = D // W_PIECES
+        windows = [held.tile([P, S], F32, name=f"window{db}") for db in range(BLOCKS)]
+        for q in range(W_PIECES):
+            nc.scalar.dma_start(
+                weights[:, :, q * piece : (q + 1) * piece], weights_dram[:, :, q * piece : (q + 1) * piece]
+            )
+            for db in range(q * BLOCKS // W_PIECES, (q + 1) * BLOCKS // W_PIECES):
+                nc.sync.dma_start(windows[db][:], base[db * P : (db + 1) * P, :])
+
+        biased = held.tile([P, BLOCKS, N], BF16, name="biased")
+        for kb in range(BLOCKS):
+            nc.vector.tensor_tensor(
+                biased[:, kb, :].rearrange("p (b m) -> p b m", b=B),
+                clusters[:, kb, :].rearrange("p (b m) -> p b m", b=B),
+                cluster_bias[:, kb, :].unsqueeze(1).to_broadcast([P, B, M]),
+                ADD,
+            )
+
+        for db in range(BLOCKS):
+            product = psum.tile([P, N], F32, name="product")
+            for kb in range(BLOCKS):
+                nc.tensor.matmul(
+                    product[:],
+                    weights[:, kb, db * P : (db + 1) * P],
+                    biased[:, kb, :],
+                    start=(kb == 0),
+                    stop=(kb == BLOCKS - 1),
+                )
+            gate = work.tile([P, N], F32, name="gate")
+            nc.scalar.activation(gate[:], product[:], SIGMOID, bias=layer_bias[:, db : db + 1])
+            z = work.tile([P, N], F32, name="z")
+            nc.scalar.activation(z[:], product[:], IDENTITY, bias=layer_bias[:, db : db + 1])
+            nc.vector.tensor_tensor(windows[db][:].indirect(offsets[:]), z[:], gate[:], MULT)
+            nc.sync.dma_start(out[db * P : (db + 1) * P, :], windows[db][:])

@@ -1,4 +1,5 @@
 import concourse.mybir as mybir
+from concourse.masks import make_identity
 
 P = 128
 D, S, B, M, N = 1024, 512, 4, 64, 256
@@ -15,33 +16,49 @@ def tile_fuzzyclustering_kernel(tc, base, value_clusters, vbias, w, bv, offs, ou
     nc = tc.nc
     with (
         tc.tile_pool(name="held", bufs=1) as held,
-        tc.tile_pool(name="work", bufs=3) as work,
-        tc.psum_pool(name="psum", bufs=3) as psum,
+        tc.tile_pool(name="work", bufs=4) as work,
+        tc.psum_pool(name="psum_once", bufs=1) as psum_once,
+        tc.psum_pool(name="psum", bufs=2) as psum,
     ):
+        scratch = held.tile([P, 1], F32, name="scratch")
+        nc.gpsimd.memset(scratch[:], 0.0)
+        warmed = held.tile([P, 1], F32, name="warmed")
+        nc.scalar.activation(warmed[:], scratch[:], SIGMOID)
+
         offsets = held.tile([P, N // 16], U16, name="offsets")
         nc.sync.dma_start(offsets[:], offs)
+        bias_rows = held.tile([BLOCKS, P], F32, name="bias_rows")
+        nc.sync.dma_start(bias_rows[:], bv.rearrange("(db p) o -> db (p o)", p=P))
 
         cluster_bias = held.tile([P, BLOCKS, M], F32, name="cluster_bias")
-        nc.scalar.dma_start(cluster_bias[:], vbias.rearrange("(kb p) m -> p kb m", p=P))
         clusters = held.tile([P, BLOCKS, N], F32, name="clusters")
-        clusters_dram = value_clusters.rearrange("(kb p) n -> p kb n", p=P)
-        for kb in range(0, BLOCKS, 2):
-            nc.sync.dma_start(clusters[:, kb : kb + 2, :], clusters_dram[:, kb : kb + 2, :])
-
-        layer_bias = held.tile([P, BLOCKS], F32, name="layer_bias")
-        with nc.allow_non_contiguous_dma(reason="1024 single floats, one for each partition and block"):
-            nc.gpsimd.dma_start(layer_bias[:], bv.rearrange("(db p) o -> p (db o)", p=P))
-
         weights = held.tile([P, BLOCKS, D], BF16, name="weights")
-        weights_dram = w.rearrange("(kb p) d -> p kb d", p=P)
-        piece = D // W_PIECES
+        clusters_dram = value_clusters.rearrange("(p kb) n -> p kb n", kb=BLOCKS)
+        weights_dram = w.rearrange("(p kb) d -> p kb d", kb=BLOCKS)
         windows = [held.tile([P, S], F32, name=f"window{db}") for db in range(BLOCKS)]
-        for q in range(W_PIECES):
-            nc.scalar.dma_start(
-                weights[:, :, q * piece : (q + 1) * piece], weights_dram[:, :, q * piece : (q + 1) * piece]
-            )
-            for db in range(q * BLOCKS // W_PIECES, (q + 1) * BLOCKS // W_PIECES):
-                nc.sync.dma_start(windows[db][:], base[db * P : (db + 1) * P, :])
+
+        def clusters_load(kb):
+            return (clusters[:, kb : kb + 2, :], clusters_dram[:, kb : kb + 2, :])
+
+        def weights_load(q):
+            columns = slice(q * (D // W_PIECES), (q + 1) * (D // W_PIECES))
+            return (weights[:, :, columns], weights_dram[:, :, columns])
+
+        def window_load(db):
+            return (windows[db][:], base[db * P : (db + 1) * P, :])
+
+        loads = [(cluster_bias[:], vbias.rearrange("(p kb) m -> p kb m", kb=BLOCKS)), clusters_load(0), weights_load(0)]
+        loads += [clusters_load(kb) for kb in range(2, BLOCKS, 2)]
+        loads += [window_load(0), window_load(1)]
+        for q in range(1, W_PIECES):
+            loads += [weights_load(q), window_load(2 * q), window_load(2 * q + 1)]
+        for tile_side, dram_side in loads:
+            nc.sync.dma_start(tile_side, dram_side)
+
+        identity = held.tile([BLOCKS, BLOCKS], F32, name="identity")
+        make_identity(nc, identity[:])
+        flipped = psum_once.tile([P, BLOCKS], F32, name="flipped")
+        nc.tensor.matmul(flipped[:], bias_rows[:], identity[:], start=True, stop=True)
 
         biased = held.tile([P, BLOCKS, N], BF16, name="biased")
         for kb in range(BLOCKS):
@@ -51,6 +68,8 @@ def tile_fuzzyclustering_kernel(tc, base, value_clusters, vbias, w, bv, offs, ou
                 cluster_bias[:, kb, :].unsqueeze(1).to_broadcast([P, B, M]),
                 ADD,
             )
+        layer_bias = held.tile([P, BLOCKS], F32, name="layer_bias")
+        nc.vector.tensor_copy(layer_bias[:], flipped[:])
 
         for db in range(BLOCKS):
             product = psum.tile([P, N], F32, name="product")

@@ -1,10 +1,11 @@
 import concourse.mybir as mybir
-from concourse.masks import make_identity
 
 P = 128
 D, S, B, M, N = 1024, 512, 4, 64, 256
 BLOCKS = D // P
-W_PIECES = 4
+SQUARE = 32
+W_PIECES = ((0, 1), (1, 2), (2, 4), (4, 6), (6, 8))
+WARM_MATMULS = 6
 FLOPS = 2 * D * D * N
 
 F32, BF16, U16 = mybir.dt.float32, mybir.dt.bfloat16, mybir.dt.uint16
@@ -20,15 +21,13 @@ def tile_fuzzyclustering_kernel(tc, base, value_clusters, vbias, w, bv, offs, ou
         tc.psum_pool(name="psum_once", bufs=1) as psum_once,
         tc.psum_pool(name="psum", bufs=2) as psum,
     ):
-        scratch = held.tile([P, 1], F32, name="scratch")
-        nc.gpsimd.memset(scratch[:], 0.0)
-        warmed = held.tile([P, 1], F32, name="warmed")
-        nc.scalar.activation(warmed[:], scratch[:], SIGMOID)
-
         offsets = held.tile([P, N // 16], U16, name="offsets")
         nc.sync.dma_start(offsets[:], offs)
-        bias_rows = held.tile([BLOCKS, P], F32, name="bias_rows")
-        nc.sync.dma_start(bias_rows[:], bv.rearrange("(db p) o -> db (p o)", p=P))
+        bias_runs = held.tile([P, SQUARE], F32, name="bias_runs", align_bytes=64)
+        nc.vector.memset(bias_runs[:], 0.0)
+        bias_runs_dram = bv.rearrange("(db g i) o -> g db (i o)", g=P // SQUARE, i=SQUARE)
+        for g in range(P // SQUARE):
+            nc.sync.dma_start(bias_runs[g * SQUARE : g * SQUARE + BLOCKS, :], bias_runs_dram[g])
 
         cluster_bias = held.tile([P, BLOCKS, M], F32, name="cluster_bias")
         clusters = held.tile([P, BLOCKS, N], F32, name="clusters")
@@ -40,25 +39,33 @@ def tile_fuzzyclustering_kernel(tc, base, value_clusters, vbias, w, bv, offs, ou
         def clusters_load(kb):
             return (clusters[:, kb : kb + 2, :], clusters_dram[:, kb : kb + 2, :])
 
-        def weights_load(q):
-            columns = slice(q * (D // W_PIECES), (q + 1) * (D // W_PIECES))
+        def weights_load(first_block, end_block):
+            columns = slice(first_block * P, end_block * P)
             return (weights[:, :, columns], weights_dram[:, :, columns])
 
         def window_load(db):
             return (windows[db][:], base[db * P : (db + 1) * P, :])
 
-        loads = [(cluster_bias[:], vbias.rearrange("(p kb) m -> p kb m", kb=BLOCKS)), clusters_load(0), weights_load(0)]
+        loads = [(cluster_bias[:], vbias.rearrange("(p kb) m -> p kb m", kb=BLOCKS)), clusters_load(0)]
+        loads += [weights_load(*W_PIECES[0])]
         loads += [clusters_load(kb) for kb in range(2, BLOCKS, 2)]
-        loads += [window_load(0), window_load(1)]
-        for q in range(1, W_PIECES):
-            loads += [weights_load(q), window_load(2 * q), window_load(2 * q + 1)]
+        loads += [window_load(0)]
+        for first_block, end_block in W_PIECES[1:]:
+            loads += [weights_load(first_block, end_block)]
+            loads += [window_load(db) for db in range(first_block, end_block)]
         for tile_side, dram_side in loads:
             nc.sync.dma_start(tile_side, dram_side)
 
-        identity = held.tile([BLOCKS, BLOCKS], F32, name="identity")
-        make_identity(nc, identity[:])
-        flipped = psum_once.tile([P, BLOCKS], F32, name="flipped")
-        nc.tensor.matmul(flipped[:], bias_rows[:], identity[:], start=True, stop=True)
+        zeros = held.tile([P, S], BF16, name="zeros")
+        nc.vector.memset(zeros[:], 0.0)
+        warmed = held.tile([P, 1], F32, name="warmed")
+        nc.scalar.activation(warmed[:], zeros[:, 0:1], SIGMOID)
+        idle_product = psum_once.tile([P, S], F32, name="idle_product")
+        for i in range(WARM_MATMULS):
+            nc.tensor.matmul(idle_product[:], zeros[:, 0:P], zeros[:], start=True, stop=True)
+
+        layer_bias = held.tile([P, SQUARE], F32, name="layer_bias", align_bytes=64)
+        nc.vector.transpose(layer_bias[:], bias_runs[:])
 
         biased = held.tile([P, BLOCKS, N], BF16, name="biased")
         for kb in range(BLOCKS):
@@ -68,8 +75,6 @@ def tile_fuzzyclustering_kernel(tc, base, value_clusters, vbias, w, bv, offs, ou
                 cluster_bias[:, kb, :].unsqueeze(1).to_broadcast([P, B, M]),
                 ADD,
             )
-        layer_bias = held.tile([P, BLOCKS], F32, name="layer_bias")
-        nc.vector.tensor_copy(layer_bias[:], flipped[:])
 
         for db in range(BLOCKS):
             product = psum.tile([P, N], F32, name="product")

@@ -4,8 +4,10 @@ P = 128
 D, S, B, M, N = 1024, 512, 4, 64, 256
 BLOCKS = D // P
 SQUARE = 32
-W_PIECES = ((0, 1), (1, 2), (2, 4), (4, 6), (6, 8))
+CLUSTER_PIECES = ((0, 2), (2, 4), (4, 6), (6, 7), (7, 8))
+W_PIECES = ((0, 2), (2, 4), (4, 6), (6, 8))
 WARM_MATMULS = 6
+FIRST_BLOCK_CUTS = 2
 FLOPS = 2 * D * D * N
 
 F32, BF16, U16 = mybir.dt.float32, mybir.dt.bfloat16, mybir.dt.uint16
@@ -23,11 +25,6 @@ def tile_fuzzyclustering_kernel(tc, base, value_clusters, vbias, w, bv, offs, ou
     ):
         offsets = held.tile([P, N // 16], U16, name="offsets")
         nc.sync.dma_start(offsets[:], offs)
-        bias_runs = held.tile([P, SQUARE], F32, name="bias_runs", align_bytes=64)
-        nc.vector.memset(bias_runs[:], 0.0)
-        bias_runs_dram = bv.rearrange("(db g i) o -> g db (i o)", g=P // SQUARE, i=SQUARE)
-        for g in range(P // SQUARE):
-            nc.sync.dma_start(bias_runs[g * SQUARE : g * SQUARE + BLOCKS, :], bias_runs_dram[g])
 
         cluster_bias = held.tile([P, BLOCKS, M], F32, name="cluster_bias")
         clusters = held.tile([P, BLOCKS, N], F32, name="clusters")
@@ -35,9 +32,12 @@ def tile_fuzzyclustering_kernel(tc, base, value_clusters, vbias, w, bv, offs, ou
         clusters_dram = value_clusters.rearrange("(p kb) n -> p kb n", kb=BLOCKS)
         weights_dram = w.rearrange("(p kb) d -> p kb d", kb=BLOCKS)
         windows = [held.tile([P, S], F32, name=f"window{db}") for db in range(BLOCKS)]
+        bias_runs = held.tile([P, SQUARE], F32, name="bias_runs", align_bytes=64)
+        nc.vector.memset(bias_runs[:], 0.0)
+        bias_runs_dram = bv.rearrange("(db g i) o -> g db (i o)", g=P // SQUARE, i=SQUARE)
 
-        def clusters_load(kb):
-            return (clusters[:, kb : kb + 2, :], clusters_dram[:, kb : kb + 2, :])
+        def clusters_load(first_group, end_group):
+            return (clusters[:, first_group:end_group, :], clusters_dram[:, first_group:end_group, :])
 
         def weights_load(first_block, end_block):
             columns = slice(first_block * P, end_block * P)
@@ -46,13 +46,15 @@ def tile_fuzzyclustering_kernel(tc, base, value_clusters, vbias, w, bv, offs, ou
         def window_load(db):
             return (windows[db][:], base[db * P : (db + 1) * P, :])
 
-        loads = [(cluster_bias[:], vbias.rearrange("(p kb) m -> p kb m", kb=BLOCKS)), clusters_load(0)]
-        loads += [weights_load(*W_PIECES[0])]
-        loads += [clusters_load(kb) for kb in range(2, BLOCKS, 2)]
+        loads = [(cluster_bias[:], vbias.rearrange("(p kb) m -> p kb m", kb=BLOCKS))]
+        loads += [clusters_load(*CLUSTER_PIECES[0]), weights_load(*W_PIECES[0])]
+        loads += [clusters_load(*piece) for piece in CLUSTER_PIECES[1:]]
+        loads += [(bias_runs[g * SQUARE : g * SQUARE + BLOCKS, :], bias_runs_dram[g]) for g in range(P // SQUARE)]
         loads += [window_load(0)]
         for first_block, end_block in W_PIECES[1:]:
             loads += [weights_load(first_block, end_block)]
-            loads += [window_load(db) for db in range(first_block, end_block)]
+            loads += [window_load(db - 1) for db in range(first_block, end_block)]
+        loads += [window_load(BLOCKS - 1)]
         for tile_side, dram_side in loads:
             nc.sync.dma_start(tile_side, dram_side)
 
@@ -64,9 +66,6 @@ def tile_fuzzyclustering_kernel(tc, base, value_clusters, vbias, w, bv, offs, ou
         for i in range(WARM_MATMULS):
             nc.tensor.matmul(idle_product[:], zeros[:, 0:P], zeros[:], start=True, stop=True)
 
-        layer_bias = held.tile([P, SQUARE], F32, name="layer_bias", align_bytes=64)
-        nc.vector.transpose(layer_bias[:], bias_runs[:])
-
         biased = held.tile([P, BLOCKS, N], BF16, name="biased")
         for kb in range(BLOCKS):
             nc.vector.tensor_tensor(
@@ -75,6 +74,9 @@ def tile_fuzzyclustering_kernel(tc, base, value_clusters, vbias, w, bv, offs, ou
                 cluster_bias[:, kb, :].unsqueeze(1).to_broadcast([P, B, M]),
                 ADD,
             )
+
+        layer_bias = held.tile([P, SQUARE], F32, name="layer_bias", align_bytes=64)
+        nc.vector.transpose(layer_bias[:], bias_runs[:])
 
         for db in range(BLOCKS):
             product = psum.tile([P, N], F32, name="product")
@@ -87,8 +89,13 @@ def tile_fuzzyclustering_kernel(tc, base, value_clusters, vbias, w, bv, offs, ou
                     stop=(kb == BLOCKS - 1),
                 )
             gate = work.tile([P, N], F32, name="gate")
-            nc.scalar.activation(gate[:], product[:], SIGMOID, bias=layer_bias[:, db : db + 1])
             z = work.tile([P, N], F32, name="z")
-            nc.scalar.activation(z[:], product[:], IDENTITY, bias=layer_bias[:, db : db + 1])
-            nc.vector.tensor_tensor(windows[db][:].indirect(offsets[:]), z[:], gate[:], MULT)
+            cuts = FIRST_BLOCK_CUTS if db == 0 else 1
+            width = N // cuts
+            for cut in range(cuts):
+                columns = slice(cut * width, (cut + 1) * width)
+                entries = offsets[:, cut * width // 16 : (cut + 1) * width // 16]
+                nc.scalar.activation(gate[:, columns], product[:, columns], SIGMOID, bias=layer_bias[:, db : db + 1])
+                nc.scalar.activation(z[:, columns], product[:, columns], IDENTITY, bias=layer_bias[:, db : db + 1])
+                nc.vector.tensor_tensor(windows[db][:].indirect(entries), z[:, columns], gate[:, columns], MULT)
             nc.sync.dma_start(out[db * P : (db + 1) * P, :], windows[db][:])

@@ -7,7 +7,6 @@ SQUARE = 32
 CLUSTER_PIECES = ((0, 2), (2, 4), (4, 6), (6, 7), (7, 8))
 W_PIECES = ((0, 2), (2, 4), (4, 6), (6, 8))
 WARM_MATMULS = 6
-FIRST_BLOCK_CUTS = 2
 FLOPS = 2 * D * D * N
 
 F32, BF16, U16 = mybir.dt.float32, mybir.dt.bfloat16, mybir.dt.uint16
@@ -89,13 +88,8 @@ def tile_fuzzyclustering_kernel(tc, base, value_clusters, vbias, w, bv, offs, ou
                     stop=(kb == BLOCKS - 1),
                 )
             gate = work.tile([P, N], F32, name="gate")
+            nc.scalar.activation(gate[:], product[:], SIGMOID, bias=layer_bias[:, db : db + 1])
             z = work.tile([P, N], F32, name="z")
-            cuts = FIRST_BLOCK_CUTS if db == 0 else 1
-            width = N // cuts
-            for cut in range(cuts):
-                columns = slice(cut * width, (cut + 1) * width)
-                entries = offsets[:, cut * width // 16 : (cut + 1) * width // 16]
-                nc.scalar.activation(gate[:, columns], product[:, columns], SIGMOID, bias=layer_bias[:, db : db + 1])
-                nc.scalar.activation(z[:, columns], product[:, columns], IDENTITY, bias=layer_bias[:, db : db + 1])
-                nc.vector.tensor_tensor(windows[db][:].indirect(entries), z[:, columns], gate[:, columns], MULT)
+            nc.scalar.activation(z[:], product[:], IDENTITY, bias=layer_bias[:, db : db + 1])
+            nc.vector.tensor_tensor(windows[db][:].indirect(offsets[:]), z[:], gate[:], MULT)
             nc.sync.dma_start(out[db * P : (db + 1) * P, :], windows[db][:])

@@ -4,8 +4,9 @@ P = 128
 D, S, B, M, N = 1024, 512, 4, 64, 256
 BLOCKS = D // P
 SQUARE = 32
-CLUSTER_PIECES = ((0, 2), (2, 4), (4, 6), (6, 7), (7, 8))
+CLUSTER_PIECES = ((0, 2), (2, 4), (4, 6), (6, 8))
 W_PIECES = ((0, 2), (2, 4), (4, 6), (6, 8))
+FIRST_W_GROUPS = ((0, 4), (4, 8))
 WARM_MATMULS = 6
 FLOPS = 2 * D * D * N
 
@@ -38,16 +39,19 @@ def tile_fuzzyclustering_kernel(tc, base, value_clusters, vbias, w, bv, offs, ou
         def clusters_load(first_group, end_group):
             return (clusters[:, first_group:end_group, :], clusters_dram[:, first_group:end_group, :])
 
-        def weights_load(first_block, end_block):
+        def weights_load(first_block, end_block, first_group=0, end_group=BLOCKS):
             columns = slice(first_block * P, end_block * P)
-            return (weights[:, :, columns], weights_dram[:, :, columns])
+            groups = slice(first_group, end_group)
+            return (weights[:, groups, columns], weights_dram[:, groups, columns])
 
         def window_load(db):
             return (windows[db][:], base[db * P : (db + 1) * P, :])
 
         loads = [(cluster_bias[:], vbias.rearrange("(p kb) m -> p kb m", kb=BLOCKS))]
-        loads += [clusters_load(*CLUSTER_PIECES[0]), weights_load(*W_PIECES[0])]
-        loads += [clusters_load(*piece) for piece in CLUSTER_PIECES[1:]]
+        loads += [clusters_load(*piece) for piece in CLUSTER_PIECES[0:2]]
+        loads += [weights_load(*W_PIECES[0], *FIRST_W_GROUPS[0])]
+        loads += [clusters_load(*piece) for piece in CLUSTER_PIECES[2:4]]
+        loads += [weights_load(*W_PIECES[0], *FIRST_W_GROUPS[1])]
         loads += [(bias_runs[g * SQUARE : g * SQUARE + BLOCKS, :], bias_runs_dram[g]) for g in range(P // SQUARE)]
         loads += [window_load(0)]
         for first_block, end_block in W_PIECES[1:]:

@@ -24,7 +24,6 @@ def tile_fuzzyclustering_kernel(tc, base, value_clusters, vbias, w, bv, offs, ou
         tc.psum_pool(name="psum", bufs=2) as psum,
     ):
         offsets = held.tile([P, N // 16], U16, name="offsets")
-        nc.sync.dma_start(offsets[:], offs)
 
         cluster_bias = held.tile([P, BLOCKS, M], F32, name="cluster_bias")
         clusters = held.tile([P, BLOCKS, N], F32, name="clusters")
@@ -53,7 +52,7 @@ def tile_fuzzyclustering_kernel(tc, base, value_clusters, vbias, w, bv, offs, ou
         loads += [clusters_load(*piece) for piece in CLUSTER_PIECES[2:4]]
         loads += [weights_load(*W_PIECES[0], *FIRST_W_GROUPS[1])]
         loads += [(bias_runs[g * SQUARE : g * SQUARE + BLOCKS, :], bias_runs_dram[g]) for g in range(P // SQUARE)]
-        loads += [window_load(0)]
+        loads += [(offsets[:], offs), window_load(0)]
         for first_block, end_block in W_PIECES[1:]:
             loads += [weights_load(first_block, end_block)]
             loads += [window_load(db - 1) for db in range(first_block, end_block)]

@@ -7,6 +7,7 @@ SQUARE = 32
 CLUSTER_PIECES = ((0, 2), (2, 4), (4, 6), (6, 8))
 W_PIECES = ((0, 2), (2, 4), (4, 6), (6, 8))
 FIRST_W_GROUPS = ((0, 4), (4, 8))
+FIRST_BLOCK_CUTS = ((0, N // 2), (N // 2, N))
 WARM_MATMULS = 6
 FLOPS = 2 * D * D * N
 
@@ -81,18 +82,28 @@ def tile_fuzzyclustering_kernel(tc, base, value_clusters, vbias, w, bv, offs, ou
         nc.vector.transpose(layer_bias[:], bias_runs[:])
 
         for db in range(BLOCKS):
-            product = psum.tile([P, N], F32, name="product")
-            for kb in range(BLOCKS):
-                nc.tensor.matmul(
-                    product[:],
-                    weights[:, kb, db * P : (db + 1) * P],
-                    biased[:, kb, :],
-                    start=(kb == 0),
-                    stop=(kb == BLOCKS - 1),
-                )
+            if db == 0:
+                parts = [
+                    (first, end, psum_once.tile([P, S], F32, name=f"first_product{first}")[:, 0 : end - first])
+                    for first, end in FIRST_BLOCK_CUTS
+                ]
+            else:
+                product = psum.tile([P, N], F32, name="product")
+                parts = [(0, N, product[:])]
+            for first_group, end_group in FIRST_W_GROUPS:
+                for first, end, part in parts:
+                    for kb in range(first_group, end_group):
+                        nc.tensor.matmul(
+                            part,
+                            weights[:, kb, db * P : (db + 1) * P],
+                            biased[:, kb, first:end],
+                            start=(kb == 0),
+                            stop=(kb == BLOCKS - 1),
+                        )
             gate = work.tile([P, N], F32, name="gate")
-            nc.scalar.activation(gate[:], product[:], SIGMOID, bias=layer_bias[:, db : db + 1])
             z = work.tile([P, N], F32, name="z")
-            nc.scalar.activation(z[:], product[:], IDENTITY, bias=layer_bias[:, db : db + 1])
+            for first, end, part in parts:
+                nc.scalar.activation(gate[:, first:end], part, SIGMOID, bias=layer_bias[:, db : db + 1])
+                nc.scalar.activation(z[:, first:end], part, IDENTITY, bias=layer_bias[:, db : db + 1])
             nc.vector.tensor_tensor(windows[db][:].indirect(offsets[:]), z[:], gate[:], MULT)
             nc.sync.dma_start(out[db * P : (db + 1) * P, :], windows[db][:])

@@ -47,13 +47,14 @@ def tile_fuzzyclustering_kernel(tc, base, value_clusters, vbias, w, bv, offs, ou
         def window_load(db):
             return (windows[db][:], base[db * P : (db + 1) * P, :])
 
+        def bias_load(g):
+            return (bias_runs[g * SQUARE : g * SQUARE + BLOCKS, :], bias_runs_dram[g])
+
         loads = [(cluster_bias[:], vbias.rearrange("(p kb) m -> p kb m", kb=BLOCKS))]
-        loads += [clusters_load(*piece) for piece in CLUSTER_PIECES[0:2]]
+        loads += [clusters_load(*CLUSTER_PIECES[0]), bias_load(0), bias_load(1), clusters_load(*CLUSTER_PIECES[1])]
         loads += [weights_load(*W_PIECES[0], *FIRST_W_GROUPS[0])]
-        loads += [clusters_load(*piece) for piece in CLUSTER_PIECES[2:4]]
-        loads += [weights_load(*W_PIECES[0], *FIRST_W_GROUPS[1])]
-        loads += [(bias_runs[g * SQUARE : g * SQUARE + BLOCKS, :], bias_runs_dram[g]) for g in range(P // SQUARE)]
-        loads += [(offsets[:], offs), window_load(0)]
+        loads += [clusters_load(*piece) for piece in CLUSTER_PIECES[2:4]] + [bias_load(2), bias_load(3)]
+        loads += [weights_load(*W_PIECES[0], *FIRST_W_GROUPS[1]), window_load(0), (offsets[:], offs)]
         for first_block, end_block in W_PIECES[1:]:
             loads += [weights_load(first_block, end_block)]
             loads += [window_load(db - 1) for db in range(first_block, end_block)]

@@ -70,12 +70,15 @@ def tile_fuzzyclustering_kernel(tc, base, value_clusters, vbias, w, bv, offs, ou
         for i in range(WARM_MATMULS):
             nc.tensor.matmul(idle_product[:], zeros[:, 0:P], zeros[:], start=True, stop=True)
 
+        last_groups = range(*CLUSTER_PIECES[-1])
+        additions = list(CLUSTER_PIECES[:-1]) + [(kb, kb + 1) for kb in last_groups]
         biased = held.tile([P, BLOCKS, N], BF16, name="biased")
-        for kb in range(BLOCKS):
+        for first_group, end_group in additions:
+            groups = slice(first_group, end_group)
             nc.vector.tensor_tensor(
-                biased[:, kb, :].rearrange("p (b m) -> p b m", b=B),
-                clusters[:, kb, :].rearrange("p (b m) -> p b m", b=B),
-                cluster_bias[:, kb, :].unsqueeze(1).to_broadcast([P, B, M]),
+                biased[:, groups, :].rearrange("p kb (b m) -> p kb b m", b=B),
+                clusters[:, groups, :].rearrange("p kb (b m) -> p kb b m", b=B),
+                cluster_bias[:, groups, :].unsqueeze(2).to_broadcast([P, end_group - first_group, B, M]),
                 ADD,
             )
 

@@ -53,12 +53,14 @@ def tile_fuzzyclustering_kernel(tc, base, value_clusters, vbias, w, bv, offs, ou
         loads = [(cluster_bias[:], vbias.rearrange("(p kb) m -> p kb m", kb=BLOCKS))]
         loads += [clusters_load(*CLUSTER_PIECES[0]), bias_load(0), bias_load(1), clusters_load(*CLUSTER_PIECES[1])]
         loads += [weights_load(*W_PIECES[0], *FIRST_W_GROUPS[0])]
-        loads += [clusters_load(*piece) for piece in CLUSTER_PIECES[2:4]] + [bias_load(2), bias_load(3)]
-        loads += [weights_load(*W_PIECES[0], *FIRST_W_GROUPS[1]), window_load(0), (offsets[:], offs)]
-        for first_block, end_block in W_PIECES[1:]:
+        loads += [clusters_load(*piece) for piece in CLUSTER_PIECES[2:4]]
+        loads += [weights_load(*W_PIECES[0], *FIRST_W_GROUPS[1]), bias_load(2), bias_load(3)]
+        loads += [window_load(0), (offsets[:], offs)]
+        for first_block, end_block in W_PIECES[1:-1]:
             loads += [weights_load(first_block, end_block)]
             loads += [window_load(db - 1) for db in range(first_block, end_block)]
-        loads += [window_load(BLOCKS - 1)]
+        loads += [weights_load(*W_PIECES[-1], *groups) for groups in FIRST_W_GROUPS]
+        loads += [window_load(db) for db in range(BLOCKS - 3, BLOCKS)]
         for tile_side, dram_side in loads:
             nc.sync.dma_start(tile_side, dram_side)
 

@@ -8,7 +8,6 @@ CLUSTER_PIECES = ((0, 2), (2, 4), (4, 6), (6, 8))
 W_PIECES = ((0, 2), (2, 4), (4, 6), (6, 8))
 FIRST_W_GROUPS = ((0, 4), (4, 8))
 FIRST_BLOCK_CUTS = ((0, N // 2), (N // 2, N))
-WARM_MATMULS = 6
 FLOPS = 2 * D * D * N
 
 F32, BF16, U16 = mybir.dt.float32, mybir.dt.bfloat16, mybir.dt.uint16
@@ -64,13 +63,9 @@ def tile_fuzzyclustering_kernel(tc, base, value_clusters, vbias, w, bv, offs, ou
         for tile_side, dram_side in loads:
             nc.sync.dma_start(tile_side, dram_side)
 
-        zeros = held.tile([P, S], BF16, name="zeros")
-        nc.vector.memset(zeros[:], 0.0)
-        warmed = held.tile([P, 1], F32, name="warmed")
-        nc.scalar.activation(warmed[:], zeros[:, 0:1], SIGMOID)
-        idle_product = psum_once.tile([P, S], F32, name="idle_product")
-        for i in range(WARM_MATMULS):
-            nc.tensor.matmul(idle_product[:], zeros[:, 0:P], zeros[:], start=True, stop=True)
+        scratch = held.tile([P, 2], F32, name="scratch")
+        nc.vector.memset(scratch[:], 0.0)
+        nc.scalar.activation(scratch[:, 1:2], scratch[:, 0:1], SIGMOID)
 
         last_groups = range(*CLUSTER_PIECES[-1])
         additions = list(CLUSTER_PIECES[:-1]) + [(kb, kb + 1) for kb in last_groups]

import concourse.mybir as mybir

P = 128
D, S, B, M, N = 1024, 512, 4, 64, 256
BLOCKS = D // P
SQUARE = 32
CLUSTER_PIECES = ((0, 2), (2, 4), (4, 6), (6, 8))
W_PIECES = ((0, 2), (2, 4), (4, 6), (6, 8))
FIRST_W_GROUPS = ((0, 4), (4, 8))
FIRST_BLOCK_CUTS = ((0, N // 2), (N // 2, N))
FLOPS = 2 * D * D * N

F32, BF16, U16 = mybir.dt.float32, mybir.dt.bfloat16, mybir.dt.uint16
ADD, MULT = mybir.AluOpType.add, mybir.AluOpType.mult
SIGMOID, IDENTITY = mybir.ActivationFunctionType.Sigmoid, mybir.ActivationFunctionType.Identity


def tile_fuzzyclustering_kernel(tc, base, value_clusters, vbias, w, bv, offs, out):
    nc = tc.nc
    with (
        tc.tile_pool(name="held", bufs=1) as held,
        tc.tile_pool(name="work", bufs=4) as work,
        tc.psum_pool(name="psum_once", bufs=1) as psum_once,
        tc.psum_pool(name="psum", bufs=2) as psum,
    ):
        offsets = held.tile([P, N // 16], U16, name="offsets")

        cluster_bias = held.tile([P, BLOCKS, M], F32, name="cluster_bias")
        clusters = held.tile([P, BLOCKS, N], F32, name="clusters")
        weights = held.tile([P, BLOCKS, D], BF16, name="weights")
        clusters_dram = value_clusters.rearrange("(p kb) n -> p kb n", kb=BLOCKS)
        weights_dram = w.rearrange("(p kb) d -> p kb d", kb=BLOCKS)
        windows = [held.tile([P, S], F32, name=f"window{db}") for db in range(BLOCKS)]
        bias_runs = held.tile([P, SQUARE], F32, name="bias_runs", align_bytes=64)
        nc.vector.memset(bias_runs[:], 0.0)
        bias_runs_dram = bv.rearrange("(db g i) o -> g db (i o)", g=P // SQUARE, i=SQUARE)

        def clusters_load(first_group, end_group):
            return (clusters[:, first_group:end_group, :], clusters_dram[:, first_group:end_group, :])

        def weights_load(first_block, end_block, first_group=0, end_group=BLOCKS):
            columns = slice(first_block * P, end_block * P)
            groups = slice(first_group, end_group)
            return (weights[:, groups, columns], weights_dram[:, groups, columns])

        def window_load(db):
            return (windows[db][:], base[db * P : (db + 1) * P, :])

        def bias_load(g):
            return (bias_runs[g * SQUARE : g * SQUARE + BLOCKS, :], bias_runs_dram[g])

        loads = [(cluster_bias[:], vbias.rearrange("(p kb) m -> p kb m", kb=BLOCKS))]
        loads += [clusters_load(*CLUSTER_PIECES[0]), bias_load(0), bias_load(1), clusters_load(*CLUSTER_PIECES[1])]
        loads += [weights_load(*W_PIECES[0], *FIRST_W_GROUPS[0])]
        loads += [clusters_load(*piece) for piece in CLUSTER_PIECES[2:4]]
        loads += [weights_load(*W_PIECES[0], *FIRST_W_GROUPS[1]), bias_load(2), bias_load(3)]
        loads += [window_load(0), (offsets[:], offs)]
        for first_block, end_block in W_PIECES[1:-1]:
            loads += [weights_load(first_block, end_block)]
            loads += [window_load(db - 1) for db in range(first_block, end_block)]
        loads += [weights_load(*W_PIECES[-1], *groups) for groups in FIRST_W_GROUPS]
        loads += [window_load(db) for db in range(BLOCKS - 3, BLOCKS)]
        for tile_side, dram_side in loads:
            nc.sync.dma_start(tile_side, dram_side)

        scratch = held.tile([P, 2], F32, name="scratch")
        nc.vector.memset(scratch[:], 0.0)
        nc.scalar.activation(scratch[:, 1:2], scratch[:, 0:1], SIGMOID)

        last_groups = range(*CLUSTER_PIECES[-1])
        additions = list(CLUSTER_PIECES[:-1]) + [(kb, kb + 1) for kb in last_groups]
        biased = held.tile([P, BLOCKS, N], BF16, name="biased")
        for first_group, end_group in additions:
            groups = slice(first_group, end_group)
            nc.vector.tensor_tensor(
                biased[:, groups, :].rearrange("p kb (b m) -> p kb b m", b=B),
                clusters[:, groups, :].rearrange("p kb (b m) -> p kb b m", b=B),
                cluster_bias[:, groups, :].unsqueeze(2).to_broadcast([P, end_group - first_group, B, M]),
                ADD,
            )

        layer_bias = held.tile([P, SQUARE], F32, name="layer_bias", align_bytes=64)
        nc.vector.transpose(layer_bias[:], bias_runs[:])

        for db in range(BLOCKS):
            if db == 0:
                parts = [
                    (first, end, psum_once.tile([P, S], F32, name=f"first_product{first}")[:, 0 : end - first])
                    for first, end in FIRST_BLOCK_CUTS
                ]
            else:
                product = psum.tile([P, N], F32, name="product")
                parts = [(0, N, product[:])]
            for first_group, end_group in FIRST_W_GROUPS:
                for first, end, part in parts:
                    for kb in range(first_group, end_group):
                        nc.tensor.matmul(
                            part,
                            weights[:, kb, db * P : (db + 1) * P],
                            biased[:, kb, first:end],
                            start=(kb == 0),
                            stop=(kb == BLOCKS - 1),
                        )
            gate = work.tile([P, N], F32, name="gate")
            z = work.tile([P, N], F32, name="z")
            for first, end, part in parts:
                nc.scalar.activation(gate[:, first:end], part, SIGMOID, bias=layer_bias[:, db : db + 1])
                nc.scalar.activation(z[:, first:end], part, IDENTITY, bias=layer_bias[:, db : db + 1])
            nc.vector.tensor_tensor(windows[db][:].indirect(offsets[:]), z[:], gate[:], MULT)
            nc.sync.dma_start(out[db * P : (db + 1) * P, :], windows[db][:])
